import numpy as np
import ml_dtypes


def mxq(x, axis, fmt="e4m3"):
    dtype, down = {"e4m3": (ml_dtypes.float8_e4m3fn, 7), "e5m2": (ml_dtypes.float8_e5m2, 14)}[fmt]
    v = np.moveaxis(np.asarray(x, np.float32).astype(ml_dtypes.bfloat16).astype(np.float64), axis, -1)
    blocks = v.reshape(v.shape[:-1] + (-1, 32))
    amax = np.abs(blocks).max(-1, keepdims=True)
    byte = np.maximum(np.where(amax > 0, np.frexp(amax)[1] - 1 + 127, 0) - down, 1)
    scale = np.exp2(byte - 127.0)
    codes = (blocks / scale).astype(np.float32).astype(dtype).astype(np.float64)
    return np.moveaxis((codes * scale).reshape(v.shape), -1, axis)


WIDE = False


def mx_kscale(k):
    if not WIDE:
        return np.ones(k)
    levels = np.array([10, -10, 5, -5, 0])
    a = np.random.permutation(np.resize(levels, k // 512 * 4)).reshape(k // 512, 4)
    idx = np.arange(k)
    return np.exp2(a[idx // 512, idx % 128 // 32])


BF16 = ml_dtypes.bfloat16


def bf(x):
    return np.asarray(x, np.float32).astype(BF16)


def f64(x):
    return np.asarray(x).astype(np.float64)


E2M1 = np.array([0.0, 0.5, 1.0, 1.5, 2.0, 3.0, 4.0, 6.0, -0.0, -0.5, -1.0, -1.5, -2.0, -3.0, -4.0, -6.0])


def pack_weight(w, fmt):
    k, n = w.shape
    w = f64(bf(w)).reshape(k // 32, 32, n)
    amax = np.abs(w).max(1)
    if fmt == "e4m3":
        byte = np.frexp(amax)[1] - 1 + 127 - 7
    else:
        mant, ex = np.frexp(amax / 6.0)
        byte = np.where(mant > 0.5, ex, ex - 1) + 127
    byte = np.clip(np.where(amax > 0, byte, 1), 1, 254)
    scaled = (w * np.exp2(127.0 - byte)[:, None, :]).reshape(k, n).astype(np.float32)
    by_word = np.ascontiguousarray(scaled.reshape(k // 512, 128, 4, n).transpose(0, 1, 3, 2))
    if fmt == "e4m3":
        words = by_word.astype(ml_dtypes.float8_e4m3fn).view(np.uint8)
    else:
        c = by_word.astype(ml_dtypes.float4_e2m1fn).view(np.uint8) & 0xF
        words = c[..., 0::2] | (c[..., 1::2] << 4)
    return np.ascontiguousarray(words), np.ascontiguousarray(byte.astype(np.uint8).reshape(k // 512, 16, n))


def unpack_weight(words, scales, fmt):
    g, p, n, _ = words.shape
    if fmt == "e4m3":
        vals = np.ascontiguousarray(words).view(ml_dtypes.float8_e4m3fn).astype(np.float64)
    else:
        nib = np.empty((g, p, n, 4), np.uint8)
        nib[..., 0::2] = words & 0xF
        nib[..., 1::2] = words >> 4
        vals = E2M1[nib]
    vals = vals * np.repeat(np.exp2(scales.astype(np.float64) - 127.0), 8, axis=1)[..., None]
    return vals.transpose(0, 1, 3, 2).reshape(g * 512, n)


B, R, C, H, DH = 2, 8, 8192, 12, 128
T = R * R
E = H * DH
EPS = 2.0 ** -23
FMT = "e4m3"


def rmsnorm(v):
    return v * (1.0 / np.sqrt(np.mean(np.square(v), axis=-1, keepdims=True) + EPS))


def setup_inputs():
    s = mx_kscale(C)
    x = bf(np.random.standard_normal((B, T, C)) * s)
    Wq_words, Wq_scales = pack_weight(np.random.standard_normal((C, E)) / np.sqrt(C) / s[:, None], FMT)
    Wk_words, Wk_scales = pack_weight(np.random.standard_normal((C, E)) / np.sqrt(C) / s[:, None], FMT)
    return {"x": x,
            "Wq_words": Wq_words, "Wq_scales": Wq_scales,
            "Wk_words": Wk_words, "Wk_scales": Wk_scales}


def reference(x, Wq_words, Wq_scales, Wk_words, Wk_scales):
    xq = mxq(f64(x), 2, "e4m3")

    def proj(words, scales):
        return (xq @ unpack_weight(words, scales, FMT)).reshape(B, T, H, DH).transpose(0, 2, 1, 3)

    return rmsnorm(proj(Wq_words, Wq_scales)), rmsnorm(proj(Wk_words, Wk_scales))

@@ -1,0 +1,182 @@
+from contextlib import ExitStack
+
+import concourse.mybir as mybir
+from concourse.masks import make_identity
+
+F32 = mybir.dt.float32
+BF16 = mybir.dt.bfloat16
+I32 = mybir.dt.int32
+U32 = mybir.dt.uint32
+U8 = mybir.dt.uint8
+FP8X4 = mybir.dt.float8_e4m3fn_x4
+ACT = mybir.ActivationFunctionType
+ALU = mybir.AluOpType
+
+P = 128
+PACK = 4
+K_GROUP = P * PACK
+C = 8192
+GROUPS = C // K_GROUP
+BOARDS = 2
+SQUARES = 64
+HEADS = 12
+DH = 128
+E = HEADS * DH
+BANK_COLS = 512
+BANKS = E // BANK_COLS
+BANK_HEADS = BANK_COLS // DH
+EPS = 2.0**-23
+
+X_PIECES = 4
+PIECE_GROUPS = GROUPS // X_PIECES
+PIECE_COLS = PIECE_GROUPS * K_GROUP
+WORDS_PER_GROUP = K_GROUP // 2
+
+QUAD = 4
+QUADS = GROUPS // QUAD
+LIVE = QUAD * QUAD
+
+RING = GROUPS
+
+FLOPS = 2 * P * C * 2 * E
+
+
+def tile_pieceroutedattention_pa_k_kernel(
+    tc, x, Wq_words, Wq_scales, Wk_words, Wk_scales, out_0, out_1
+):
+    nc = tc.nc
+    x_flat = x.flatten_outer_dims()
+
+    with ExitStack() as ctx:
+        keep = ctx.enter_context(tc.tile_pool(name="keep", bufs=1))
+        grouped_pool = ctx.enter_context(tc.tile_pool(name="grouped", bufs=2))
+        ring = ctx.enter_context(tc.tile_pool(name="ring", bufs=RING))
+        norm_pool = ctx.enter_context(tc.tile_pool(name="norm", bufs=BANKS))
+        flip_psum = ctx.enter_context(tc.psum_pool(name="flip", bufs=2))
+        acc_psum = ctx.enter_context(tc.psum_pool(name="acc", bufs=1))
+        ctx.enter_context(tc.manual_schedule())
+
+        ident = keep.tile([P, P], F32, name="ident")
+        make_identity(nc, ident[:])
+        eps = keep.tile([P, 1], F32, name="eps")
+        nc.vector.memset(eps[:], EPS)
+
+        x_codes = keep.tile([P, GROUPS * P], U32, name="x_codes", align_bytes=64)
+        x_scales = keep.tile([P, GROUPS * P], U8, name="x_scales", align_bytes=64)
+
+        planes = {}
+        for name in ("q", "k"):
+            planes[name] = keep.tile([P, QUADS, E], U8, name="planes_" + name, align_bytes=64)
+            nc.vector.memset(planes[name][:].bitcast(I32), 0)
+
+        x_rows = []
+        for piece in range(X_PIECES):
+            rows = keep.tile([P, PIECE_COLS], BF16, name="x_rows_%d" % piece)
+            cols = slice(piece * PIECE_COLS, (piece + 1) * PIECE_COLS)
+            nc.sync.dma_start(out=rows[:], in_=x_flat[:, cols])
+            x_rows.append(rows)
+
+        def load_scales(name, scales):
+            for quad in range(QUADS):
+                for q4 in range(QUAD):
+                    nc.sync.dma_start(
+                        out=planes[name][32 * q4 : 32 * q4 + LIVE, quad, :].bitcast(I32),
+                        in_=scales[
+                            QUAD * quad : QUAD * (quad + 1), QUAD * q4 : QUAD * (q4 + 1), :
+                        ].bitcast(I32),
+                    )
+
+        def quantise_piece(piece):
+            words = x_rows[piece][:].bitcast(F32)
+            grouped = grouped_pool.tile(
+                [P, PIECE_GROUPS, P, PACK], BF16, name="grouped", align_bytes=64
+            )
+            grouped_words = grouped[:].bitcast(F32)
+            for half in range(2):
+                flipped = flip_psum.tile([P, 2, 2, P], F32, name="flipped")
+                for local in range(2):
+                    first = (2 * half + local) * WORDS_PER_GROUP
+                    for u in range(2):
+                        nc.tensor.transpose(
+                            flipped[:, local, u, :],
+                            words[:, first + u : first + WORDS_PER_GROUP : 2],
+                            ident[:],
+                        )
+                copy_out = nc.vector.tensor_copy if half == 0 else nc.scalar.copy
+                copy_out(
+                    out=grouped_words[:, 2 * half : 2 * half + 2, :, :],
+                    in_=flipped[:].rearrange("p g u r -> p g r u"),
+                )
+            cols = slice(piece * PIECE_GROUPS * P, (piece + 1) * PIECE_GROUPS * P)
+            nc.vector.quantize_mx(
+                out=x_codes[:, cols].bitcast(FP8X4),
+                scales=x_scales[:, cols],
+                in_=grouped[:].rearrange("p g r t -> p (g r t)"),
+            )
+
+        def project(name, words, acc):
+            for g in range(GROUPS):
+                w_words = ring.tile([P, E], U32, name="w_words", align_bytes=64)
+                nc.sync.dma_start(
+                    out=w_words[:].bitcast(I32),
+                    in_=words[g].rearrange("p n t -> p (n t)").bitcast(I32),
+                )
+                quad, j = divmod(g, QUAD)
+                tokens = slice(g * P, (g + 1) * P)
+                for bank in range(BANKS):
+                    cols = slice(bank * BANK_COLS, (bank + 1) * BANK_COLS)
+                    nc.tensor.matmul_mx(
+                        out=acc[bank][:],
+                        lhsT=x_codes[:, tokens].bitcast(FP8X4),
+                        lhsT_scale=x_scales[:, tokens],
+                        rhs=w_words[:, cols].bitcast(FP8X4),
+                        rhs_scale=planes[name][QUAD * j : P, quad, cols],
+                        start=(g == 0),
+                        stop=(g == GROUPS - 1),
+                    )
+
+        def normalise_and_store(acc_bank, out, bank, queue):
+            squares = norm_pool.tile([P, BANK_COLS], F32, name="squares")
+            sumsq = norm_pool.tile([P, BANK_HEADS], F32, name="sumsq")
+            for h in range(BANK_HEADS):
+                cols = slice(h * DH, (h + 1) * DH)
+                nc.scalar.activation(
+                    out=squares[:, cols],
+                    in_=acc_bank[:, cols],
+                    func=ACT.Square,
+                    accum_out=sumsq[:, h : h + 1],
+                )
+            rms = norm_pool.tile([P, BANK_HEADS], F32, name="rms")
+            nc.scalar.activation(
+                out=rms[:], in_=sumsq[:], func=ACT.Sqrt, scale=1.0 / DH, bias=eps[:]
+            )
+            inv_rms = norm_pool.tile([P, BANK_HEADS], F32, name="inv_rms")
+            nc.vector.reciprocal(out=inv_rms[:], in_=rms[:])
+            normed = norm_pool.tile([P, BANK_HEADS, DH], F32, name="normed")
+            nc.vector.tensor_tensor(
+                out=normed[:],
+                in0=acc_bank[:].rearrange("p (h d) -> p h d", h=BANK_HEADS),
+                in1=inv_rms[:].unsqueeze(2).to_broadcast([P, BANK_HEADS, DH]),
+                op=ALU.mult,
+            )
+            heads = slice(bank * BANK_HEADS, (bank + 1) * BANK_HEADS)
+            for b in range(BOARDS):
+                queue.dma_start(
+                    out=out[b, heads, :, :].rearrange("h t d -> t h d"),
+                    in_=normed[b * SQUARES : (b + 1) * SQUARES, :, :],
+                )
+
+        load_scales("q", Wq_scales)
+        for piece in range(X_PIECES):
+            quantise_piece(piece)
+
+        acc_q = [acc_psum.tile([P, BANK_COLS], F32, name="acc_q%d" % b) for b in range(BANKS)]
+        acc_k = [acc_psum.tile([P, BANK_COLS], F32, name="acc_k%d" % b) for b in range(BANKS)]
+
+        project("q", Wq_words, acc_q)
+        load_scales("k", Wk_scales)
+        for bank in range(BANKS):
+            normalise_and_store(acc_q[bank], out_0, bank, nc.gpsimd)
+        project("k", Wk_words, acc_k)
+        for bank in range(BANKS):
+            normalise_and_store(acc_k[bank], out_1, bank, nc.sync)

@@ -79,11 +79,11 @@ def tile_pieceroutedattention_pa_k_kernel(
         def load_scales(name, scales):
             for quad in range(QUADS):
                 for q4 in range(QUAD):
-                    nc.sync.dma_start(
-                        out=planes[name][32 * q4 : 32 * q4 + LIVE, quad, :].bitcast(I32),
+                    nc.gpsimd.dma_start(
+                        out=planes[name][32 * q4 : 32 * q4 + LIVE, quad, :].bitcast(F32),
                         in_=scales[
                             QUAD * quad : QUAD * (quad + 1), QUAD * q4 : QUAD * (q4 + 1), :
-                        ].bitcast(I32),
+                        ].bitcast(F32),
                     )
 
         def quantise_piece(piece):
@@ -167,6 +167,7 @@ def tile_pieceroutedattention_pa_k_kernel(
                 )
 
         load_scales("q", Wq_scales)
+        load_scales("k", Wk_scales)
         for piece in range(X_PIECES):
             quantise_piece(piece)
 
@@ -174,7 +175,6 @@ def tile_pieceroutedattention_pa_k_kernel(
         acc_k = [acc_psum.tile([P, BANK_COLS], F32, name="acc_k%d" % b) for b in range(BANKS)]
 
         project("q", Wq_words, acc_q)
-        load_scales("k", Wk_scales)
         for bank in range(BANKS):
             normalise_and_store(acc_q[bank], out_0, bank, nc.gpsimd)
         project("k", Wk_words, acc_k)

@@ -51,7 +51,7 @@ def tile_pieceroutedattention_pa_k_kernel(
         keep = ctx.enter_context(tc.tile_pool(name="keep", bufs=1))
         grouped_pool = ctx.enter_context(tc.tile_pool(name="grouped", bufs=2))
         ring = ctx.enter_context(tc.tile_pool(name="ring", bufs=RING))
-        norm_pool = ctx.enter_context(tc.tile_pool(name="norm", bufs=BANKS))
+        norm_pool = ctx.enter_context(tc.tile_pool(name="norm", bufs=2 * BANKS))
         flip_psum = ctx.enter_context(tc.psum_pool(name="flip", bufs=2))
         acc_psum = ctx.enter_context(tc.psum_pool(name="acc", bufs=1))
         ctx.enter_context(tc.manual_schedule())
@@ -135,7 +135,7 @@ def tile_pieceroutedattention_pa_k_kernel(
                         stop=(g == GROUPS - 1),
                     )
 
-        def normalise_and_store(acc_bank, out, bank, queue):
+        def normalise(acc_bank):
             squares = norm_pool.tile([P, BANK_COLS], F32, name="squares")
             sumsq = norm_pool.tile([P, BANK_HEADS], F32, name="sumsq")
             for h in range(BANK_HEADS):
@@ -159,9 +159,12 @@ def tile_pieceroutedattention_pa_k_kernel(
                 in1=inv_rms[:].unsqueeze(2).to_broadcast([P, BANK_HEADS, DH]),
                 op=ALU.mult,
             )
+            return normed
+
+        def store(normed, out, bank):
             heads = slice(bank * BANK_HEADS, (bank + 1) * BANK_HEADS)
             for b in range(BOARDS):
-                queue.dma_start(
+                nc.sync.dma_start(
                     out=out[b, heads, :, :].rearrange("h t d -> t h d"),
                     in_=normed[b * SQUARES : (b + 1) * SQUARES, :, :],
                 )
@@ -175,8 +178,9 @@ def tile_pieceroutedattention_pa_k_kernel(
         acc_k = [acc_psum.tile([P, BANK_COLS], F32, name="acc_k%d" % b) for b in range(BANKS)]
 
         project("q", Wq_words, acc_q)
-        for bank in range(BANKS):
-            normalise_and_store(acc_q[bank], out_0, bank, nc.gpsimd)
+        normed_q = [normalise(acc_q[bank]) for bank in range(BANKS)]
         project("k", Wk_words, acc_k)
         for bank in range(BANKS):
-            normalise_and_store(acc_k[bank], out_1, bank, nc.sync)
+            store(normed_q[bank], out_0, bank)
+        for bank in range(BANKS):
+            store(normalise(acc_k[bank]), out_1, bank)

@@ -18,7 +18,6 @@ K_GROUP = P * PACK
 C = 8192
 GROUPS = C // K_GROUP
 BOARDS = 2
-SQUARES = 64
 HEADS = 12
 DH = 128
 E = HEADS * DH
@@ -45,7 +44,6 @@ def tile_pieceroutedattention_pa_k_kernel(
     tc, x, Wq_words, Wq_scales, Wk_words, Wk_scales, out_0, out_1
 ):
     nc = tc.nc
-    x_flat = x.flatten_outer_dims()
 
     with ExitStack() as ctx:
         keep = ctx.enter_context(tc.tile_pool(name="keep", bufs=1))
@@ -73,7 +71,8 @@ def tile_pieceroutedattention_pa_k_kernel(
         for piece in range(X_PIECES):
             rows = keep.tile([P, PIECE_COLS], BF16, name="x_rows_%d" % piece)
             cols = slice(piece * PIECE_COLS, (piece + 1) * PIECE_COLS)
-            nc.sync.dma_start(out=rows[:], in_=x_flat[:, cols])
+            for b in range(BOARDS):
+                nc.sync.dma_start(out=rows[b:P:BOARDS, :], in_=x[b, :, cols])
             x_rows.append(rows)
 
         def load_scales(name, scales):
@@ -166,7 +165,7 @@ def tile_pieceroutedattention_pa_k_kernel(
             for b in range(BOARDS):
                 nc.sync.dma_start(
                     out=out[b, heads, :, :].rearrange("h t d -> t h d"),
-                    in_=normed[b * SQUARES : (b + 1) * SQUARES, :, :],
+                    in_=normed[b:P:BOARDS, :, :],
                 )
 
         load_scales("q", Wq_scales)

@@ -56,6 +56,11 @@ def tile_pieceroutedattention_pa_k_kernel(
 
         ident = keep.tile([P, P], F32, name="ident")
         make_identity(nc, ident[:])
+        perm = keep.tile([P, P], F32, name="perm")
+        nc.vector.tensor_copy(
+            out=perm[:].rearrange("p (t b) -> p b t", b=BOARDS),
+            in_=ident[:].rearrange("p (b t) -> p b t", b=BOARDS),
+        )
         eps = keep.tile([P, 1], F32, name="eps")
         nc.vector.memset(eps[:], EPS)
 
@@ -71,8 +76,7 @@ def tile_pieceroutedattention_pa_k_kernel(
         for piece in range(X_PIECES):
             rows = keep.tile([P, PIECE_COLS], BF16, name="x_rows_%d" % piece)
             cols = slice(piece * PIECE_COLS, (piece + 1) * PIECE_COLS)
-            for b in range(BOARDS):
-                nc.sync.dma_start(out=rows[b:P:BOARDS, :], in_=x[b, :, cols])
+            nc.sync.dma_start(out=rows[:], in_=x.rearrange("b t c -> (b t) c")[:, cols])
             x_rows.append(rows)
 
         def load_scales(name, scales):
@@ -99,7 +103,7 @@ def tile_pieceroutedattention_pa_k_kernel(
                         nc.tensor.transpose(
                             flipped[:, local, u, :],
                             words[:, first + u : first + WORDS_PER_GROUP : 2],
-                            ident[:],
+                            perm[:],
                         )
                 copy_out = nc.vector.tensor_copy if half == 0 else nc.scalar.copy
                 copy_out(

@@ -120,10 +120,13 @@ def tile_pieceroutedattention_pa_k_kernel(
         def project(name, words, acc):
             for g in range(GROUPS):
                 w_words = ring.tile([P, E], U32, name="w_words", align_bytes=64)
-                nc.sync.dma_start(
-                    out=w_words[:].bitcast(I32),
-                    in_=words[g].rearrange("p n t -> p (n t)").bitcast(I32),
-                )
+                flat = words[g].rearrange("p n t -> p (n t)")
+                width = BANK_COLS if (name == "k" and g == GROUPS - 1) else E
+                for lo in range(0, E, width):
+                    nc.sync.dma_start(
+                        out=w_words[:, lo : lo + width].bitcast(I32),
+                        in_=flat[:, PACK * lo : PACK * (lo + width)].bitcast(I32),
+                    )
                 quad, j = divmod(g, QUAD)
                 tokens = slice(g * P, (g + 1) * P)
                 for bank in range(BANKS):
@@ -149,12 +152,14 @@ def tile_pieceroutedattention_pa_k_kernel(
                     func=ACT.Square,
                     accum_out=sumsq[:, h : h + 1],
                 )
-            rms = norm_pool.tile([P, BANK_HEADS], F32, name="rms")
-            nc.scalar.activation(
-                out=rms[:], in_=sumsq[:], func=ACT.Sqrt, scale=1.0 / DH, bias=eps[:]
-            )
             inv_rms = norm_pool.tile([P, BANK_HEADS], F32, name="inv_rms")
-            nc.vector.reciprocal(out=inv_rms[:], in_=rms[:])
+            nc.scalar.activation(
+                out=inv_rms[:],
+                in_=sumsq[:],
+                func=ACT.Abs_reciprocal_sqrt,
+                scale=1.0 / DH,
+                bias=eps[:],
+            )
             normed = norm_pool.tile([P, BANK_HEADS, DH], F32, name="normed")
             nc.vector.tensor_tensor(
                 out=normed[:],

@@ -35,6 +35,8 @@ QUAD = 4
 QUADS = GROUPS // QUAD
 LIVE = QUAD * QUAD
 
+DMA_ALIGN = 2048
+
 RING = GROUPS
 
 FLOPS = 2 * P * C * 2 * E
@@ -69,12 +71,16 @@ def tile_pieceroutedattention_pa_k_kernel(
 
         planes = {}
         for name in ("q", "k"):
-            planes[name] = keep.tile([P, QUADS, E], U8, name="planes_" + name, align_bytes=64)
+            planes[name] = keep.tile(
+                [P, QUADS, E], U8, name="planes_" + name, align_bytes=DMA_ALIGN
+            )
             nc.vector.memset(planes[name][:].bitcast(I32), 0)
 
         x_rows = []
         for piece in range(X_PIECES):
-            rows = keep.tile([P, PIECE_COLS], BF16, name="x_rows_%d" % piece)
+            rows = keep.tile(
+                [P, PIECE_COLS], BF16, name="x_rows_%d" % piece, align_bytes=DMA_ALIGN
+            )
             cols = slice(piece * PIECE_COLS, (piece + 1) * PIECE_COLS)
             nc.sync.dma_start(out=rows[:], in_=x.rearrange("b t c -> (b t) c")[:, cols])
             x_rows.append(rows)
@@ -119,7 +125,7 @@ def tile_pieceroutedattention_pa_k_kernel(
 
         def project(name, words, acc):
             for g in range(GROUPS):
-                w_words = ring.tile([P, E], U32, name="w_words", align_bytes=64)
+                w_words = ring.tile([P, E], U32, name="w_words", align_bytes=DMA_ALIGN)
                 flat = words[g].rearrange("p n t -> p (n t)")
                 width = BANK_COLS if (name == "k" and g == GROUPS - 1) else E
                 for lo in range(0, E, width):
@@ -160,7 +166,9 @@ def tile_pieceroutedattention_pa_k_kernel(
                 scale=1.0 / DH,
                 bias=eps[:],
             )
-            normed = norm_pool.tile([P, BANK_HEADS, DH], F32, name="normed")
+            normed = norm_pool.tile(
+                [P, BANK_HEADS, DH], F32, name="normed", align_bytes=DMA_ALIGN
+            )
             nc.vector.tensor_tensor(
                 out=normed[:],
                 in0=acc_bank[:].rearrange("p (h d) -> p h d", h=BANK_HEADS),

@@ -35,7 +35,7 @@ QUAD = 4
 QUADS = GROUPS // QUAD
 LIVE = QUAD * QUAD
 
-DMA_ALIGN = 2048
+DMA_ALIGN = 256
 
 RING = GROUPS
 

from contextlib import ExitStack

import concourse.mybir as mybir
from concourse.masks import make_identity

F32 = mybir.dt.float32
BF16 = mybir.dt.bfloat16
I32 = mybir.dt.int32
U32 = mybir.dt.uint32
U8 = mybir.dt.uint8
FP8X4 = mybir.dt.float8_e4m3fn_x4
ACT = mybir.ActivationFunctionType
ALU = mybir.AluOpType

P = 128
PACK = 4
K_GROUP = P * PACK
C = 8192
GROUPS = C // K_GROUP
BOARDS = 2
HEADS = 12
DH = 128
E = HEADS * DH
BANK_COLS = 512
BANKS = E // BANK_COLS
BANK_HEADS = BANK_COLS // DH
EPS = 2.0**-23

X_PIECES = 4
PIECE_GROUPS = GROUPS // X_PIECES
PIECE_COLS = PIECE_GROUPS * K_GROUP
WORDS_PER_GROUP = K_GROUP // 2

QUAD = 4
QUADS = GROUPS // QUAD
LIVE = QUAD * QUAD

DMA_ALIGN = 256

RING = GROUPS

FLOPS = 2 * P * C * 2 * E


def tile_pieceroutedattention_pa_k_kernel(
    tc, x, Wq_words, Wq_scales, Wk_words, Wk_scales, out_0, out_1
):
    nc = tc.nc

    with ExitStack() as ctx:
        keep = ctx.enter_context(tc.tile_pool(name="keep", bufs=1))
        grouped_pool = ctx.enter_context(tc.tile_pool(name="grouped", bufs=2))
        ring = ctx.enter_context(tc.tile_pool(name="ring", bufs=RING))
        norm_pool = ctx.enter_context(tc.tile_pool(name="norm", bufs=2 * BANKS))
        flip_psum = ctx.enter_context(tc.psum_pool(name="flip", bufs=2))
        acc_psum = ctx.enter_context(tc.psum_pool(name="acc", bufs=1))
        ctx.enter_context(tc.manual_schedule())

        ident = keep.tile([P, P], F32, name="ident")
        make_identity(nc, ident[:])
        perm = keep.tile([P, P], F32, name="perm")
        nc.vector.tensor_copy(
            out=perm[:].rearrange("p (t b) -> p b t", b=BOARDS),
            in_=ident[:].rearrange("p (b t) -> p b t", b=BOARDS),
        )
        eps = keep.tile([P, 1], F32, name="eps")
        nc.vector.memset(eps[:], EPS)

        x_codes = keep.tile([P, GROUPS * P], U32, name="x_codes", align_bytes=64)
        x_scales = keep.tile([P, GROUPS * P], U8, name="x_scales", align_bytes=64)

        planes = {}
        for name in ("q", "k"):
            planes[name] = keep.tile(
                [P, QUADS, E], U8, name="planes_" + name, align_bytes=DMA_ALIGN
            )
            nc.vector.memset(planes[name][:].bitcast(I32), 0)

        x_rows = []
        for piece in range(X_PIECES):
            rows = keep.tile(
                [P, PIECE_COLS], BF16, name="x_rows_%d" % piece, align_bytes=DMA_ALIGN
            )
            cols = slice(piece * PIECE_COLS, (piece + 1) * PIECE_COLS)
            nc.sync.dma_start(out=rows[:], in_=x.rearrange("b t c -> (b t) c")[:, cols])
            x_rows.append(rows)

        def load_scales(name, scales):
            for quad in range(QUADS):
                for q4 in range(QUAD):
                    nc.gpsimd.dma_start(
                        out=planes[name][32 * q4 : 32 * q4 + LIVE, quad, :].bitcast(F32),
                        in_=scales[
                            QUAD * quad : QUAD * (quad + 1), QUAD * q4 : QUAD * (q4 + 1), :
                        ].bitcast(F32),
                    )

        def quantise_piece(piece):
            words = x_rows[piece][:].bitcast(F32)
            grouped = grouped_pool.tile(
                [P, PIECE_GROUPS, P, PACK], BF16, name="grouped", align_bytes=64
            )
            grouped_words = grouped[:].bitcast(F32)
            for half in range(2):
                flipped = flip_psum.tile([P, 2, 2, P], F32, name="flipped")
                for local in range(2):
                    first = (2 * half + local) * WORDS_PER_GROUP
                    for u in range(2):
                        nc.tensor.transpose(
                            flipped[:, local, u, :],
                            words[:, first + u : first + WORDS_PER_GROUP : 2],
                            perm[:],
                        )
                copy_out = nc.vector.tensor_copy if half == 0 else nc.scalar.copy
                copy_out(
                    out=grouped_words[:, 2 * half : 2 * half + 2, :, :],
                    in_=flipped[:].rearrange("p g u r -> p g r u"),
                )
            cols = slice(piece * PIECE_GROUPS * P, (piece + 1) * PIECE_GROUPS * P)
            nc.vector.quantize_mx(
                out=x_codes[:, cols].bitcast(FP8X4),
                scales=x_scales[:, cols],
                in_=grouped[:].rearrange("p g r t -> p (g r t)"),
            )

        def project(name, words, acc):
            for g in range(GROUPS):
                w_words = ring.tile([P, E], U32, name="w_words", align_bytes=DMA_ALIGN)
                flat = words[g].rearrange("p n t -> p (n t)")
                width = BANK_COLS if (name == "k" and g == GROUPS - 1) else E
                for lo in range(0, E, width):
                    nc.sync.dma_start(
                        out=w_words[:, lo : lo + width].bitcast(I32),
                        in_=flat[:, PACK * lo : PACK * (lo + width)].bitcast(I32),
                    )
                quad, j = divmod(g, QUAD)
                tokens = slice(g * P, (g + 1) * P)
                for bank in range(BANKS):
                    cols = slice(bank * BANK_COLS, (bank + 1) * BANK_COLS)
                    nc.tensor.matmul_mx(
                        out=acc[bank][:],
                        lhsT=x_codes[:, tokens].bitcast(FP8X4),
                        lhsT_scale=x_scales[:, tokens],
                        rhs=w_words[:, cols].bitcast(FP8X4),
                        rhs_scale=planes[name][QUAD * j : P, quad, cols],
                        start=(g == 0),
                        stop=(g == GROUPS - 1),
                    )

        def normalise(acc_bank):
            squares = norm_pool.tile([P, BANK_COLS], F32, name="squares")
            sumsq = norm_pool.tile([P, BANK_HEADS], F32, name="sumsq")
            for h in range(BANK_HEADS):
                cols = slice(h * DH, (h + 1) * DH)
                nc.scalar.activation(
                    out=squares[:, cols],
                    in_=acc_bank[:, cols],
                    func=ACT.Square,
                    accum_out=sumsq[:, h : h + 1],
                )
            inv_rms = norm_pool.tile([P, BANK_HEADS], F32, name="inv_rms")
            nc.scalar.activation(
                out=inv_rms[:],
                in_=sumsq[:],
                func=ACT.Abs_reciprocal_sqrt,
                scale=1.0 / DH,
                bias=eps[:],
            )
            normed = norm_pool.tile(
                [P, BANK_HEADS, DH], F32, name="normed", align_bytes=DMA_ALIGN
            )
            nc.vector.tensor_tensor(
                out=normed[:],
                in0=acc_bank[:].rearrange("p (h d) -> p h d", h=BANK_HEADS),
                in1=inv_rms[:].unsqueeze(2).to_broadcast([P, BANK_HEADS, DH]),
                op=ALU.mult,
            )
            return normed

        def store(normed, out, bank):
            heads = slice(bank * BANK_HEADS, (bank + 1) * BANK_HEADS)
            for b in range(BOARDS):
                nc.sync.dma_start(
                    out=out[b, heads, :, :].rearrange("h t d -> t h d"),
                    in_=normed[b:P:BOARDS, :, :],
                )

        load_scales("q", Wq_scales)
        load_scales("k", Wk_scales)
        for piece in range(X_PIECES):
            quantise_piece(piece)

        acc_q = [acc_psum.tile([P, BANK_COLS], F32, name="acc_q%d" % b) for b in range(BANKS)]
        acc_k = [acc_psum.tile([P, BANK_COLS], F32, name="acc_k%d" % b) for b in range(BANKS)]

        project("q", Wq_words, acc_q)
        normed_q = [normalise(acc_q[bank]) for bank in range(BANKS)]
        project("k", Wk_words, acc_k)
        for bank in range(BANKS):
            store(normed_q[bank], out_0, bank)
        for bank in range(BANKS):
            store(normalise(acc_k[bank]), out_1, bank)
